import numpy as np
import ml_dtypes


def mxq(x, axis, fmt="e4m3"):
    dtype, down = {"e4m3": (ml_dtypes.float8_e4m3fn, 7), "e5m2": (ml_dtypes.float8_e5m2, 14)}[fmt]
    v = np.moveaxis(np.asarray(x, np.float32).astype(ml_dtypes.bfloat16).astype(np.float64), axis, -1)
    blocks = v.reshape(v.shape[:-1] + (-1, 32))
    amax = np.abs(blocks).max(-1, keepdims=True)
    byte = np.maximum(np.where(amax > 0, np.frexp(amax)[1] - 1 + 127, 0) - down, 1)
    scale = np.exp2(byte - 127.0)
    codes = (blocks / scale).astype(np.float32).astype(dtype).astype(np.float64)
    return np.moveaxis((codes * scale).reshape(v.shape), -1, axis)


WIDE = False


def mx_kscale(k):
    if not WIDE:
        return np.ones(k)
    levels = np.array([10, -10, 5, -5, 0])
    a = np.random.permutation(np.resize(levels, k // 512 * 4)).reshape(k // 512, 4)
    idx = np.arange(k)
    return np.exp2(a[idx // 512, idx % 128 // 32])


BF16 = ml_dtypes.bfloat16


def bf(x):
    return np.asarray(x, np.float32).astype(BF16)


def f64(x):
    return np.asarray(x).astype(np.float64)


E2M1 = np.array([0.0, 0.5, 1.0, 1.5, 2.0, 3.0, 4.0, 6.0, -0.0, -0.5, -1.0, -1.5, -2.0, -3.0, -4.0, -6.0])


def pack_weight(w, fmt):
    k, n = w.shape
    w = f64(bf(w)).reshape(k // 32, 32, n)
    amax = np.abs(w).max(1)
    if fmt == "e4m3":
        byte = np.frexp(amax)[1] - 1 + 127 - 7
    else:
        mant, ex = np.frexp(amax / 6.0)
        byte = np.where(mant > 0.5, ex, ex - 1) + 127
    byte = np.clip(np.where(amax > 0, byte, 1), 1, 254)
    scaled = (w * np.exp2(127.0 - byte)[:, None, :]).reshape(k, n).astype(np.float32)
    by_word = np.ascontiguousarray(scaled.reshape(k // 512, 128, 4, n).transpose(0, 1, 3, 2))
    if fmt == "e4m3":
        words = by_word.astype(ml_dtypes.float8_e4m3fn).view(np.uint8)
    else:
        c = by_word.astype(ml_dtypes.float4_e2m1fn).view(np.uint8) & 0xF
        words = c[..., 0::2] | (c[..., 1::2] << 4)
    return np.ascontiguousarray(words), np.ascontiguousarray(byte.astype(np.uint8).reshape(k // 512, 16, n))


def unpack_weight(words, scales, fmt):
    g, p, n, _ = words.shape
    if fmt == "e4m3":
        vals = np.ascontiguousarray(words).view(ml_dtypes.float8_e4m3fn).astype(np.float64)
    else:
        nib = np.empty((g, p, n, 4), np.uint8)
        nib[..., 0::2] = words & 0xF
        nib[..., 1::2] = words >> 4
        vals = E2M1[nib]
    vals = vals * np.repeat(np.exp2(scales.astype(np.float64) - 127.0), 8, axis=1)[..., None]
    return vals.transpose(0, 1, 3, 2).reshape(g * 512, n)


B, T, D, H, HD, F = 2, 512, 1024, 16, 64, 4096
A = H * HD
EPS = 1e-5
ERF_H = 0.5
ERF_N = 14
FMT = "e4m3"


def layernorm(x, g, b):
    mu = np.mean(x, axis=-1, keepdims=True)
    var = np.mean(np.square(x - mu), axis=-1, keepdims=True)
    return (x - mu) / np.sqrt(var + EPS) * g + b


def erf(z):
    acc = np.zeros_like(z)
    for n in range(ERF_N):
        tn = (n + 0.5) * ERF_H
        acc = acc + np.exp(-tn * tn) / (tn * tn + z * z)
    return np.tanh(np.pi * z / ERF_H) - 2.0 * ERF_H * z * np.exp(-z * z) / np.pi * acc


def gelu_erf(v):
    return 0.5 * v * (1.0 + erf(v / np.sqrt(2.0)))


def setup_inputs():
    s, t = mx_kscale(A), mx_kscale(D)
    attn = bf(np.random.standard_normal((B, T, A)) * 0.25 * s)
    x = bf(np.random.standard_normal((B, T, D)) + 0.5 * np.random.standard_normal((B, T, 1)))
    w_out_words, w_out_scales = pack_weight(np.random.standard_normal((A, D)) * 2.0 / np.sqrt(A) / s[:, None], FMT)
    b_out = bf(0.1 * np.random.standard_normal(D))
    ln2_g = bf((1.0 + 0.1 * np.random.standard_normal(D)) * t)
    ln2_b = bf(0.1 * np.random.standard_normal(D) * t)
    w1_words, w1_scales = pack_weight(np.random.standard_normal((D, F)) / np.sqrt(D) / t[:, None], FMT)
    b1 = bf(0.2 * np.random.standard_normal(F))
    return {"attn": attn,
            "x": x,
            "w_out_words": w_out_words,
            "w_out_scales": w_out_scales,
            "b_out": b_out,
            "ln2_g": ln2_g,
            "ln2_b": ln2_b,
            "w1_words": w1_words,
            "w1_scales": w1_scales,
            "b1": b1}


def reference(attn, x, w_out_words, w_out_scales, b_out, ln2_g, ln2_b, w1_words, w1_scales, b1):
    x_mid = f64(x) + ((mxq(f64(attn), 2, "e4m3") @ unpack_weight(w_out_words, w_out_scales, FMT)) + f64(b_out))
    h2 = layernorm(x_mid, f64(ln2_g), f64(ln2_b))
    hid = gelu_erf((mxq(h2, 2, "e4m3") @ unpack_weight(w1_words, w1_scales, FMT)) + f64(b1))
    return x_mid, hid

@@ -1,0 +1,226 @@
+from contextlib import ExitStack
+
+import concourse.mybir as mybir
+from concourse.masks import make_identity
+
+F32 = mybir.dt.float32
+BF16 = mybir.dt.bfloat16
+I32 = mybir.dt.int32
+U32 = mybir.dt.uint32
+U8 = mybir.dt.uint8
+FP8X4 = mybir.dt.float8_e4m3fn_x4
+ALU = mybir.AluOpType
+ACT = mybir.ActivationFunctionType
+
+P = 128
+TOKENS = 1024
+TILES = TOKENS // P
+D = 1024
+F = 4096
+K_PASS = 512
+PASSES = D // K_PASS
+BANK = 512
+Z_COLS = 2048
+EPS = 1e-5
+
+FLOPS = 2 * TOKENS * D * (D + F)
+
+
+def tile_transformerblock_pb_kernel(
+    tc, attn, x, w_out_words, w_out_scales, b_out, ln2_g, ln2_b, w1_words, w1_scales, b1, out_0, out_1
+):
+    nc = tc.nc
+
+    attn_v = attn.flatten_outer_dims().rearrange("(p i) k -> p i k", i=TILES)
+    x_v = x.flatten_outer_dims().rearrange("(p i) k -> p i k", i=TILES)
+    xmid_v = out_0.flatten_outer_dims().rearrange("(p i) n -> p i n", i=TILES)
+    hid_v = out_1.flatten_outer_dims().rearrange("(p i) n -> p i n", i=TILES)
+
+    with ExitStack() as stack:
+        keep = stack.enter_context(tc.tile_pool(name="keep", bufs=1))
+        work = stack.enter_context(tc.tile_pool(name="work", bufs=2))
+        stats = stack.enter_context(tc.tile_pool(name="stats", bufs=4))
+        zpool = stack.enter_context(tc.tile_pool(name="zpool", bufs=5))
+        psum_t = stack.enter_context(tc.psum_pool(name="psum_t", bufs=2))
+        psum_mid = stack.enter_context(tc.psum_pool(name="psum_mid", bufs=2))
+        psum_up = stack.enter_context(tc.psum_pool(name="psum_up", bufs=4))
+        stack.enter_context(tc.manual_schedule())
+
+        attn_sb = keep.tile([P, TILES, D], BF16)
+        x_sb = keep.tile([P, TILES, D], BF16)
+        wo_sb = keep.tile([P, PASSES, D], I32, align_bytes=64)
+        w1_sb = keep.tile([P, PASSES, F], I32, align_bytes=64)
+        wo_planes = keep.tile([P, D], U8, align_bytes=64)
+        w1_planes = keep.tile([P, F], U8, align_bytes=64)
+        bo_bc = keep.tile([P, D], BF16)
+        g_bc = keep.tile([P, D], BF16)
+        b_bc = keep.tile([P, D], BF16)
+        b1_bc = keep.tile([P, F], BF16)
+        a_codes = keep.tile([P, TILES, PASSES * P], U32, align_bytes=64)
+        a_planes = keep.tile([P, TILES, PASSES * P], U8, align_bytes=64)
+        h_codes = keep.tile([P, TILES, PASSES * P], U32, align_bytes=64)
+        h_planes = keep.tile([P, TILES, PASSES * P], U8, align_bytes=64)
+        ident = keep.tile([P, P], F32)
+        neg_half = keep.tile([P, 1], F32)
+
+        make_identity(nc, ident[:])
+        nc.gpsimd.memset(neg_half[:], -0.5)
+        nc.vector.memset(wo_planes[:].bitcast(I32), 0)
+        nc.vector.memset(w1_planes[:].bitcast(I32), 0)
+
+        def load_planes(planes, scales):
+            for q in range(4):
+                nc.sync.dma_start(
+                    out=planes[32 * q : 32 * q + 4 * PASSES, :].bitcast(I32),
+                    in_=scales[:, 4 * q : 4 * q + 4, :].bitcast(I32),
+                )
+
+        def load_words(words_sb, words, g, cols):
+            nc.sync.dma_start(
+                out=words_sb[:, g, cols],
+                in_=words[g].rearrange("p n t -> p (n t)").bitcast(I32)[:, cols],
+            )
+
+        def load_tokens(tiles):
+            nc.sync.dma_start(out=attn_sb[:, tiles, :], in_=attn_v[:, tiles, :])
+            nc.sync.dma_start(out=x_sb[:, tiles, :], in_=x_v[:, tiles, :])
+
+        load_tokens(slice(0, 2))
+        load_planes(wo_planes, w_out_scales)
+        for g in range(PASSES):
+            load_words(wo_sb, w_out_words, g, slice(0, D))
+        nc.sync.dma_start(out=bo_bc[:], in_=b_out.partition_broadcast(P))
+        load_tokens(slice(2, 4))
+        nc.sync.dma_start(out=g_bc[:], in_=ln2_g.partition_broadcast(P))
+        nc.sync.dma_start(out=b_bc[:], in_=ln2_b.partition_broadcast(P))
+        load_planes(w1_planes, w1_scales)
+        for g in range(PASSES):
+            load_words(w1_sb, w1_words, g, slice(0, F // 2))
+        nc.sync.dma_start(out=b1_bc[:], in_=b1.partition_broadcast(P))
+        for g in range(PASSES):
+            load_words(w1_sb, w1_words, g, slice(F // 2, F))
+        load_tokens(slice(4, TILES))
+
+        def transpose_rows(rows):
+            words = rows.bitcast(F32)
+            tp = psum_t.tile([P, PASSES, 2, P], F32)
+            for g in range(PASSES):
+                for u in range(2):
+                    nc.tensor.transpose(tp[:, g, u, :], words[:, 256 * g + u : 256 * (g + 1) : 2], ident[:])
+            return tp
+
+        def regroup(tp):
+            grouped = work.tile([P, PASSES, P, 4], BF16, align_bytes=64, bufs=4)
+            nc.scalar.copy(out=grouped[:].bitcast(F32), in_=tp[:].rearrange("p g u r -> p g r u"))
+            return grouped
+
+        def quantise(grouped, codes, planes):
+            nc.vector.quantize_mx(
+                out=codes.bitcast(FP8X4), scales=planes, in_=grouped[:].rearrange("p g r t -> p (g r t)")
+            )
+
+        def mx_product(acc, codes, planes, w_sb, w_planes, cols):
+            for g in range(PASSES):
+                nc.tensor.matmul_mx(
+                    out=acc,
+                    lhsT=codes[:, g * P : (g + 1) * P].bitcast(FP8X4),
+                    lhsT_scale=planes[:, g * P : (g + 1) * P],
+                    rhs=w_sb[:, g, cols].bitcast(FP8X4),
+                    rhs_scale=w_planes[4 * g : P, cols],
+                    start=(g == 0),
+                    stop=(g == PASSES - 1),
+                )
+
+        xb_of = {}
+        scaled_of = {}
+        rstd_of = {}
+        h2_of = {}
+        z_of = {}
+
+        def add_bias_to_residual(i):
+            xb = work.tile([P, D], F32, bufs=3)
+            nc.gpsimd.tensor_tensor(out=xb[:], in0=x_sb[:, i, :], in1=bo_bc[:], op=ALU.add)
+            xb_of[i] = xb
+
+        def project(i):
+            xmid = work.tile([P, D], F32, bufs=3)
+            sums = stats.tile([P, D // BANK], F32)
+            for h in range(D // BANK):
+                cols = slice(h * BANK, (h + 1) * BANK)
+                acc = psum_mid.tile([P, BANK], F32)
+                mx_product(acc[:], a_codes[:, i, :], a_planes[:, i, :], wo_sb, wo_planes, cols)
+                nc.vector.scalar_tensor_tensor(
+                    out=xmid[:, cols], in0=acc[:], scalar=0.0, in1=xb_of[i][:, cols],
+                    op0=ALU.add, op1=ALU.add, accum_out=sums[:, h : h + 1],
+                )
+            nc.sync.dma_start(out=xmid_v[:, i, :], in_=xmid[:])
+            neg_mean = stats.tile([P, 1], F32)
+            nc.vector.tensor_scalar(
+                out=neg_mean[:], in0=sums[:, 0:1], scalar1=sums[:, 1:2], scalar2=-1.0 / D,
+                op0=ALU.add, op1=ALU.mult,
+            )
+            squares = work.tile([P, D], BF16)
+            ssq = stats.tile([P, 1], F32)
+            nc.scalar.activation(out=squares[:], in_=xmid[:], func=ACT.Square, bias=neg_mean[:], accum_out=ssq[:])
+
+            scaled = work.tile([P, D], F32, bufs=3)
+            nc.gpsimd.tensor_scalar(
+                out=scaled[:], in0=xmid[:], scalar1=neg_mean[:], scalar2=1.0, op0=ALU.add, op1=ALU.mult
+            )
+            nc.gpsimd.tensor_tensor(out=scaled[:], in0=scaled[:], in1=g_bc[:], op=ALU.mult)
+            var_eps = stats.tile([P, 1], F32)
+            nc.gpsimd.tensor_scalar(
+                out=var_eps[:], in0=ssq[:], scalar1=1.0 / D, scalar2=EPS, op0=ALU.mult, op1=ALU.add
+            )
+            rstd = stats.tile([P, 1], F32)
+            nc.gpsimd.tensor_tensor(out=rstd[:], in0=var_eps[:], in1=neg_half[:], op=ALU.pow)
+            scaled_of[i] = scaled
+            rstd_of[i] = rstd
+
+        def finish_norm(i):
+            h2 = work.tile([P, D], BF16)
+            nc.vector.scalar_tensor_tensor(
+                out=h2[:], in0=scaled_of[i][:], scalar=rstd_of[i][:], in1=b_bc[:], op0=ALU.mult, op1=ALU.add
+            )
+            h2_of[i] = h2
+
+        def up_project(i, half):
+            z = zpool.tile([P, Z_COLS], F32)
+            for c in range(Z_COLS // BANK):
+                cols = slice(half * Z_COLS + c * BANK, half * Z_COLS + (c + 1) * BANK)
+                acc = psum_up.tile([P, BANK], F32)
+                mx_product(acc[:], h_codes[:, i, :], h_planes[:, i, :], w1_sb, w1_planes, cols)
+                nc.vector.tensor_tensor(
+                    out=z[:, c * BANK : (c + 1) * BANK], in0=acc[:], in1=b1_bc[:, cols], op=ALU.add
+                )
+            z_of[(i, half)] = z
+
+        def gelu_and_store(i, half):
+            z = z_of[(i, half)]
+            nc.scalar.activation(out=z[:], in_=z[:], func=ACT.Gelu)
+            nc.sync.dma_start(out=hid_v[:, i, half * Z_COLS : (half + 1) * Z_COLS], in_=z[:])
+
+        def is_tile(i):
+            return 0 <= i < TILES
+
+        for s in range(-1, TILES + 3):
+            tp_h = transpose_rows(h2_of[s - 2][:]) if is_tile(s - 2) else None
+            tp_a = transpose_rows(attn_sb[:, s + 1, :]) if is_tile(s + 1) else None
+            grouped_h = regroup(tp_h) if is_tile(s - 2) else None
+            grouped_a = regroup(tp_a) if is_tile(s + 1) else None
+            if is_tile(s - 3):
+                gelu_and_store(s - 3, 1)
+            if is_tile(s - 2):
+                quantise(grouped_h, h_codes[:, s - 2, :], h_planes[:, s - 2, :])
+            if is_tile(s + 1):
+                quantise(grouped_a, a_codes[:, s + 1, :], a_planes[:, s + 1, :])
+                add_bias_to_residual(s + 1)
+            if is_tile(s):
+                project(s)
+            if is_tile(s - 2):
+                up_project(s - 2, 0)
+                gelu_and_store(s - 2, 0)
+            if is_tile(s - 1):
+                finish_norm(s - 1)
+            if is_tile(s - 2):
+                up_project(s - 2, 1)

@@ -61,10 +61,15 @@ def tile_transformerblock_pb_kernel(
         h_codes = keep.tile([P, TILES, PASSES * P], U32, align_bytes=64)
         h_planes = keep.tile([P, TILES, PASSES * P], U8, align_bytes=64)
         ident = keep.tile([P, P], F32)
+        ident_bf = keep.tile([P, P], BF16)
         neg_half = keep.tile([P, 1], F32)
+        vec_rows = keep.tile([P, BANK], BF16)
+        B1_ROW, BO_ROW, G_ROW, B_ROW = 0, 8, 10, 12
 
         make_identity(nc, ident[:])
+        make_identity(nc, ident_bf[:])
         nc.gpsimd.memset(neg_half[:], -0.5)
+        nc.vector.memset(vec_rows[:], 0.0)
         nc.vector.memset(wo_planes[:].bitcast(I32), 0)
         nc.vector.memset(w1_planes[:].bitcast(I32), 0)
 
@@ -85,21 +90,38 @@ def tile_transformerblock_pb_kernel(
             nc.sync.dma_start(out=attn_sb[:, tiles, :], in_=attn_v[:, tiles, :])
             nc.sync.dma_start(out=x_sb[:, tiles, :], in_=x_v[:, tiles, :])
 
+        def load_vector(first_row, vector):
+            rows = vector.rearrange("(r c) -> r c", c=BANK)
+            nc.scalar.dma_start(out=vec_rows[first_row : first_row + rows.shape[0], :], in_=rows)
+
+        load_vector(BO_ROW, b_out)
+        load_vector(G_ROW, ln2_g)
+        load_vector(B_ROW, ln2_b)
+        load_vector(B1_ROW, b1)
         load_tokens(slice(0, 2))
         load_planes(wo_planes, w_out_scales)
         for g in range(PASSES):
             load_words(wo_sb, w_out_words, g, slice(0, D))
-        nc.sync.dma_start(out=bo_bc[:], in_=b_out.partition_broadcast(P))
         load_tokens(slice(2, 4))
-        nc.sync.dma_start(out=g_bc[:], in_=ln2_g.partition_broadcast(P))
-        nc.sync.dma_start(out=b_bc[:], in_=ln2_b.partition_broadcast(P))
         load_planes(w1_planes, w1_scales)
-        for g in range(PASSES):
-            load_words(w1_sb, w1_words, g, slice(0, F // 2))
-        nc.sync.dma_start(out=b1_bc[:], in_=b1.partition_broadcast(P))
-        for g in range(PASSES):
-            load_words(w1_sb, w1_words, g, slice(F // 2, F))
-        load_tokens(slice(4, TILES))
+        for half in range(2):
+            for g in range(PASSES):
+                load_words(w1_sb, w1_words, g, slice(half * F // 2, (half + 1) * F // 2))
+        load_tokens(slice(4, 6))
+        load_tokens(slice(6, TILES))
+
+        def spread(first_row, dest):
+            for j in range(dest.shape[1] // BANK):
+                r = first_row + j
+                acc = psum_up.tile([P, BANK], F32, tag="up")
+                nc.tensor.matmul(
+                    out=acc[:], lhsT=ident_bf[:, r : r + 1].to_broadcast([P, P]), rhs=vec_rows[:],
+                    start=True, stop=True,
+                )
+                if r % 2 == 0:
+                    nc.scalar.copy(out=dest[:, j * BANK : (j + 1) * BANK], in_=acc[:])
+                else:
+                    nc.vector.tensor_copy(out=dest[:, j * BANK : (j + 1) * BANK], in_=acc[:])
 
         def transpose_rows(rows):
             words = rows.bitcast(F32)
@@ -188,7 +210,7 @@ def tile_transformerblock_pb_kernel(
             z = zpool.tile([P, Z_COLS], F32)
             for c in range(Z_COLS // BANK):
                 cols = slice(half * Z_COLS + c * BANK, half * Z_COLS + (c + 1) * BANK)
-                acc = psum_up.tile([P, BANK], F32)
+                acc = psum_up.tile([P, BANK], F32, tag="up")
                 mx_product(acc[:], h_codes[:, i, :], h_planes[:, i, :], w1_sb, w1_planes, cols)
                 nc.vector.tensor_tensor(
                     out=z[:, c * BANK : (c + 1) * BANK], in0=acc[:], in1=b1_bc[:, cols], op=ALU.add
@@ -203,6 +225,7 @@ def tile_transformerblock_pb_kernel(
         def is_tile(i):
             return 0 <= i < TILES
 
+        spread(BO_ROW, bo_bc)
         for s in range(-1, TILES + 3):
             tp_h = transpose_rows(h2_of[s - 2][:]) if is_tile(s - 2) else None
             tp_a = transpose_rows(attn_sb[:, s + 1, :]) if is_tile(s + 1) else None
@@ -224,3 +247,8 @@ def tile_transformerblock_pb_kernel(
                 finish_norm(s - 1)
             if is_tile(s - 2):
                 up_project(s - 2, 1)
+            if s == -1:
+                spread(G_ROW, g_bc)
+                spread(B_ROW, b_bc)
+            if s == 0:
+                spread(B1_ROW, b1_bc)

@@ -177,9 +177,10 @@ def tile_transformerblock_pb_kernel(
                 )
             nc.sync.dma_start(out=xmid_v[:, i, :], in_=xmid[:])
             neg_mean = stats.tile([P, 1], F32)
+            parts = stats.tile([P, D // BANK], F32)
             nc.vector.tensor_scalar(
-                out=neg_mean[:], in0=sums[:, 0:1], scalar1=sums[:, 1:2], scalar2=-1.0 / D,
-                op0=ALU.add, op1=ALU.mult,
+                out=parts[:], in0=sums[:], scalar1=-1.0 / D, scalar2=None, op0=ALU.mult, op1=ALU.add,
+                accum_out=neg_mean[:],
             )
             squares = work.tile([P, D], BF16)
             ssq = stats.tile([P, 1], F32)
@@ -206,15 +207,17 @@ def tile_transformerblock_pb_kernel(
             )
             h2_of[i] = h2
 
-        def up_project(i, half):
+        def up_project(i, half, by_bank=False):
             z = zpool.tile([P, Z_COLS], F32)
             for c in range(Z_COLS // BANK):
                 cols = slice(half * Z_COLS + c * BANK, half * Z_COLS + (c + 1) * BANK)
+                z_cols = z[:, c * BANK : (c + 1) * BANK]
                 acc = psum_up.tile([P, BANK], F32, tag="up")
                 mx_product(acc[:], h_codes[:, i, :], h_planes[:, i, :], w1_sb, w1_planes, cols)
-                nc.vector.tensor_tensor(
-                    out=z[:, c * BANK : (c + 1) * BANK], in0=acc[:], in1=b1_bc[:, cols], op=ALU.add
-                )
+                nc.vector.tensor_tensor(out=z_cols, in0=acc[:], in1=b1_bc[:, cols], op=ALU.add)
+                if by_bank:
+                    nc.scalar.activation(out=z_cols, in_=z_cols, func=ACT.Gelu)
+                    nc.sync.dma_start(out=hid_v[:, i, cols], in_=z_cols)
             z_of[(i, half)] = z
 
         def gelu_and_store(i, half):
@@ -225,13 +228,15 @@ def tile_transformerblock_pb_kernel(
         def is_tile(i):
             return 0 <= i < TILES
 
+        LAST = TILES - 1
+
         spread(BO_ROW, bo_bc)
         for s in range(-1, TILES + 3):
             tp_h = transpose_rows(h2_of[s - 2][:]) if is_tile(s - 2) else None
             tp_a = transpose_rows(attn_sb[:, s + 1, :]) if is_tile(s + 1) else None
             grouped_h = regroup(tp_h) if is_tile(s - 2) else None
             grouped_a = regroup(tp_a) if is_tile(s + 1) else None
-            if is_tile(s - 3):
+            if is_tile(s - 3) and s - 3 != LAST:
                 gelu_and_store(s - 3, 1)
             if is_tile(s - 2):
                 quantise(grouped_h, h_codes[:, s - 2, :], h_planes[:, s - 2, :])
@@ -241,12 +246,13 @@ def tile_transformerblock_pb_kernel(
             if is_tile(s):
                 project(s)
             if is_tile(s - 2):
-                up_project(s - 2, 0)
-                gelu_and_store(s - 2, 0)
+                up_project(s - 2, 0, by_bank=(s - 2 == LAST))
+                if s - 2 != LAST:
+                    gelu_and_store(s - 2, 0)
             if is_tile(s - 1):
                 finish_norm(s - 1)
             if is_tile(s - 2):
-                up_project(s - 2, 1)
+                up_project(s - 2, 1, by_bank=(s - 2 == LAST))
             if s == -1:
                 spread(G_ROW, g_bc)
                 spread(B_ROW, b_bc)

@@ -154,6 +154,8 @@ def tile_transformerblock_pb_kernel(
                 )
 
         xb_of = {}
+        xmid_of = {}
+        sums_of = {}
         scaled_of = {}
         rstd_of = {}
         h2_of = {}
@@ -176,6 +178,12 @@ def tile_transformerblock_pb_kernel(
                     op0=ALU.add, op1=ALU.add, accum_out=sums[:, h : h + 1],
                 )
             nc.sync.dma_start(out=xmid_v[:, i, :], in_=xmid[:])
+            xmid_of[i] = xmid
+            sums_of[i] = sums
+
+        def statistics(i):
+            xmid = xmid_of[i]
+            sums = sums_of[i]
             neg_mean = stats.tile([P, 1], F32)
             parts = stats.tile([P, D // BANK], F32)
             nc.vector.tensor_scalar(
@@ -207,7 +215,7 @@ def tile_transformerblock_pb_kernel(
             )
             h2_of[i] = h2
 
-        def up_project(i, half, by_bank=False):
+        def up_project(i, half, by_bank=False, after_first_bank=None):
             z = zpool.tile([P, Z_COLS], F32)
             for c in range(Z_COLS // BANK):
                 cols = slice(half * Z_COLS + c * BANK, half * Z_COLS + (c + 1) * BANK)
@@ -218,6 +226,8 @@ def tile_transformerblock_pb_kernel(
                 if by_bank:
                     nc.scalar.activation(out=z_cols, in_=z_cols, func=ACT.Gelu)
                     nc.sync.dma_start(out=hid_v[:, i, cols], in_=z_cols)
+                if c == 0 and after_first_bank is not None:
+                    after_first_bank()
             z_of[(i, half)] = z
 
         def gelu_and_store(i, half):
@@ -245,8 +255,13 @@ def tile_transformerblock_pb_kernel(
                 add_bias_to_residual(s + 1)
             if is_tile(s):
                 project(s)
+            if is_tile(s) and not is_tile(s - 2):
+                statistics(s)
             if is_tile(s - 2):
-                up_project(s - 2, 0, by_bank=(s - 2 == LAST))
+                up_project(
+                    s - 2, 0, by_bank=(s - 2 == LAST),
+                    after_first_bank=(lambda: statistics(s)) if is_tile(s) else None,
+                )
                 if s - 2 != LAST:
                     gelu_and_store(s - 2, 0)
             if is_tile(s - 1):

@@ -66,6 +66,8 @@ def tile_transformerblock_pb_kernel(
         vec_rows = keep.tile([P, BANK], BF16)
         B1_ROW, BO_ROW, G_ROW, B_ROW = 0, 8, 10, 12
 
+        zeros = keep.tile([P, BANK], BF16)
+        nc.vector.memset(zeros[:], 0.0)
         make_identity(nc, ident[:])
         make_identity(nc, ident_bf[:])
         nc.gpsimd.memset(neg_half[:], -0.5)
@@ -86,39 +88,50 @@ def tile_transformerblock_pb_kernel(
                 in_=words[g].rearrange("p n t -> p (n t)").bitcast(I32)[:, cols],
             )
 
-        def load_tokens(tiles):
+        def load_attn(tiles):
             nc.sync.dma_start(out=attn_sb[:, tiles, :], in_=attn_v[:, tiles, :])
+
+        def load_x(tiles):
             nc.sync.dma_start(out=x_sb[:, tiles, :], in_=x_v[:, tiles, :])
 
         def load_vector(first_row, vector):
             rows = vector.rearrange("(r c) -> r c", c=BANK)
-            nc.scalar.dma_start(out=vec_rows[first_row : first_row + rows.shape[0], :], in_=rows)
+            nc.sync.dma_start(out=vec_rows[first_row : first_row + rows.shape[0], :], in_=rows)
 
+        load_attn(slice(0, 2))
         load_vector(BO_ROW, b_out)
         load_vector(G_ROW, ln2_g)
         load_vector(B_ROW, ln2_b)
         load_vector(B1_ROW, b1)
-        load_tokens(slice(0, 2))
+        load_x(slice(0, 2))
         load_planes(wo_planes, w_out_scales)
         for g in range(PASSES):
             load_words(wo_sb, w_out_words, g, slice(0, D))
-        load_tokens(slice(2, 4))
+        load_x(slice(2, 4))
+        load_attn(slice(2, 4))
         load_planes(w1_planes, w1_scales)
         for half in range(2):
             for g in range(PASSES):
                 load_words(w1_sb, w1_words, g, slice(half * F // 2, (half + 1) * F // 2))
-        load_tokens(slice(4, 6))
-        load_tokens(slice(6, TILES))
+        load_attn(slice(4, 6))
+        load_x(slice(4, 6))
+        load_attn(slice(6, TILES))
+        load_x(slice(6, TILES))
 
-        def spread(first_row, dest):
-            for j in range(dest.shape[1] // BANK):
+        def warm_up(count):
+            for n in range(count):
+                acc = psum_up.tile([P, BANK], F32, tag="up")
+                nc.tensor.matmul(out=acc[:], lhsT=zeros[:, 0:P], rhs=zeros[:], start=True, stop=True)
+
+        def spread(first_row, dest, banks, scalar_only=False):
+            for j in banks:
                 r = first_row + j
                 acc = psum_up.tile([P, BANK], F32, tag="up")
                 nc.tensor.matmul(
                     out=acc[:], lhsT=ident_bf[:, r : r + 1].to_broadcast([P, P]), rhs=vec_rows[:],
                     start=True, stop=True,
                 )
-                if r % 2 == 0:
+                if r % 2 == 0 or scalar_only:
                     nc.scalar.copy(out=dest[:, j * BANK : (j + 1) * BANK], in_=acc[:])
                 else:
                     nc.vector.tensor_copy(out=dest[:, j * BANK : (j + 1) * BANK], in_=acc[:])
@@ -153,17 +166,27 @@ def tile_transformerblock_pb_kernel(
                     stop=(g == PASSES - 1),
                 )
 
+        LAST = TILES - 1
+        RESIDUAL_ON_VECTOR = (0,)
+        CENTRE_ON_VECTOR = (0,)
+        BY_BANK_FROM = (LAST, 0)
+
         xb_of = {}
         xmid_of = {}
         sums_of = {}
+        neg_mean_of = {}
+        ssq_of = {}
         scaled_of = {}
         rstd_of = {}
         h2_of = {}
+        grouped_of = {}
         z_of = {}
+        acc_of = {}
 
         def add_bias_to_residual(i):
             xb = work.tile([P, D], F32, bufs=3)
-            nc.gpsimd.tensor_tensor(out=xb[:], in0=x_sb[:, i, :], in1=bo_bc[:], op=ALU.add)
+            engine = nc.vector if i in RESIDUAL_ON_VECTOR else nc.gpsimd
+            engine.tensor_tensor(out=xb[:], in0=x_sb[:, i, :], in1=bo_bc[:], op=ALU.add)
             xb_of[i] = xb
 
         def project(i):
@@ -181,31 +204,45 @@ def tile_transformerblock_pb_kernel(
             xmid_of[i] = xmid
             sums_of[i] = sums
 
-        def statistics(i):
-            xmid = xmid_of[i]
-            sums = sums_of[i]
+        def negative_mean(i):
             neg_mean = stats.tile([P, 1], F32)
             parts = stats.tile([P, D // BANK], F32)
             nc.vector.tensor_scalar(
-                out=parts[:], in0=sums[:], scalar1=-1.0 / D, scalar2=None, op0=ALU.mult, op1=ALU.add,
+                out=parts[:], in0=sums_of[i][:], scalar1=-1.0 / D, scalar2=None, op0=ALU.mult, op1=ALU.add,
                 accum_out=neg_mean[:],
             )
+            neg_mean_of[i] = neg_mean
+
+        def sum_of_squares(i):
             squares = work.tile([P, D], BF16)
             ssq = stats.tile([P, 1], F32)
-            nc.scalar.activation(out=squares[:], in_=xmid[:], func=ACT.Square, bias=neg_mean[:], accum_out=ssq[:])
-
-            scaled = work.tile([P, D], F32, bufs=3)
-            nc.gpsimd.tensor_scalar(
-                out=scaled[:], in0=xmid[:], scalar1=neg_mean[:], scalar2=1.0, op0=ALU.add, op1=ALU.mult
+            nc.scalar.activation(
+                out=squares[:], in_=xmid_of[i][:], func=ACT.Square, bias=neg_mean_of[i][:], accum_out=ssq[:]
             )
-            nc.gpsimd.tensor_tensor(out=scaled[:], in0=scaled[:], in1=g_bc[:], op=ALU.mult)
+            ssq_of[i] = ssq
+
+        def centre_and_scale(i):
+            scaled = work.tile([P, D], F32, bufs=3)
+            if i in CENTRE_ON_VECTOR:
+                nc.vector.scalar_tensor_tensor(
+                    out=scaled[:], in0=xmid_of[i][:], scalar=neg_mean_of[i][:], in1=g_bc[:],
+                    op0=ALU.add, op1=ALU.mult,
+                )
+            else:
+                nc.gpsimd.tensor_scalar(
+                    out=scaled[:], in0=xmid_of[i][:], scalar1=neg_mean_of[i][:], scalar2=1.0,
+                    op0=ALU.add, op1=ALU.mult,
+                )
+                nc.gpsimd.tensor_tensor(out=scaled[:], in0=scaled[:], in1=g_bc[:], op=ALU.mult)
+            scaled_of[i] = scaled
+
+        def inverse_deviation(i):
             var_eps = stats.tile([P, 1], F32)
             nc.gpsimd.tensor_scalar(
-                out=var_eps[:], in0=ssq[:], scalar1=1.0 / D, scalar2=EPS, op0=ALU.mult, op1=ALU.add
+                out=var_eps[:], in0=ssq_of[i][:], scalar1=1.0 / D, scalar2=EPS, op0=ALU.mult, op1=ALU.add
             )
             rstd = stats.tile([P, 1], F32)
             nc.gpsimd.tensor_tensor(out=rstd[:], in0=var_eps[:], in1=neg_half[:], op=ALU.pow)
-            scaled_of[i] = scaled
             rstd_of[i] = rstd
 
         def finish_norm(i):
@@ -215,22 +252,37 @@ def tile_transformerblock_pb_kernel(
             )
             h2_of[i] = h2
 
-        def up_project(i, half, by_bank=False, after_first_bank=None):
-            z = zpool.tile([P, Z_COLS], F32)
-            for c in range(Z_COLS // BANK):
-                cols = slice(half * Z_COLS + c * BANK, half * Z_COLS + (c + 1) * BANK)
-                z_cols = z[:, c * BANK : (c + 1) * BANK]
-                acc = psum_up.tile([P, BANK], F32, tag="up")
-                mx_product(acc[:], h_codes[:, i, :], h_planes[:, i, :], w1_sb, w1_planes, cols)
-                nc.vector.tensor_tensor(out=z_cols, in0=acc[:], in1=b1_bc[:, cols], op=ALU.add)
-                if by_bank:
-                    nc.scalar.activation(out=z_cols, in_=z_cols, func=ACT.Gelu)
-                    nc.sync.dma_start(out=hid_v[:, i, cols], in_=z_cols)
-                if c == 0 and after_first_bank is not None:
-                    after_first_bank()
-            z_of[(i, half)] = z
+        def turn_h2(i):
+            grouped_of[i] = regroup(transpose_rows(h2_of[i][:]))
+
+        def quantise_h2(i):
+            quantise(grouped_of[i], h_codes[:, i, :], h_planes[:, i, :])
+
+        def up_passes(i, c):
+            acc = psum_up.tile([P, BANK], F32, tag="up")
+            mx_product(acc[:], h_codes[:, i, :], h_planes[:, i, :], w1_sb, w1_planes, slice(c * BANK, (c + 1) * BANK))
+            acc_of[(i, c)] = acc
+
+        def add_b1(i, c):
+            half, quarter = divmod(c, Z_COLS // BANK)
+            if quarter == 0:
+                z = zpool.tile([P, Z_COLS], F32)
+                z_of[(i, half)] = z
+            z = z_of[(i, half)]
+            cols = slice(c * BANK, (c + 1) * BANK)
+            z_cols = z[:, quarter * BANK : (quarter + 1) * BANK]
+            nc.vector.tensor_tensor(out=z_cols, in0=acc_of[(i, c)][:], in1=b1_bc[:, cols], op=ALU.add)
+            if (i, c) >= BY_BANK_FROM:
+                nc.scalar.activation(out=z_cols, in_=z_cols, func=ACT.Gelu)
+                nc.sync.dma_start(out=hid_v[:, i, cols], in_=z_cols)
+
+        def up_bank(i, c):
+            up_passes(i, c)
+            add_b1(i, c)
 
         def gelu_and_store(i, half):
+            if (i, half * (Z_COLS // BANK)) >= BY_BANK_FROM:
+                return
             z = z_of[(i, half)]
             nc.scalar.activation(out=z[:], in_=z[:], func=ACT.Gelu)
             nc.sync.dma_start(out=hid_v[:, i, half * Z_COLS : (half + 1) * Z_COLS], in_=z[:])
@@ -238,38 +290,62 @@ def tile_transformerblock_pb_kernel(
         def is_tile(i):
             return 0 <= i < TILES
 
-        LAST = TILES - 1
+        def turn_attn(i):
+            return regroup(transpose_rows(attn_sb[:, i, :]))
 
-        spread(BO_ROW, bo_bc)
-        for s in range(-1, TILES + 3):
-            tp_h = transpose_rows(h2_of[s - 2][:]) if is_tile(s - 2) else None
-            tp_a = transpose_rows(attn_sb[:, s + 1, :]) if is_tile(s + 1) else None
-            grouped_h = regroup(tp_h) if is_tile(s - 2) else None
-            grouped_a = regroup(tp_a) if is_tile(s + 1) else None
-            if is_tile(s - 3) and s - 3 != LAST:
-                gelu_and_store(s - 3, 1)
-            if is_tile(s - 2):
-                quantise(grouped_h, h_codes[:, s - 2, :], h_planes[:, s - 2, :])
+        def quantise_attn(i, grouped):
+            quantise(grouped, a_codes[:, i, :], a_planes[:, i, :])
+
+        warm_up(5)
+        quantise_attn(0, turn_attn(0))
+        spread(BO_ROW, bo_bc, range(2))
+        for i in range(3):
+            add_bias_to_residual(i)
+        quantise_attn(1, turn_attn(1))
+        spread(G_ROW, g_bc, range(2))
+        spread(B_ROW, b_bc, range(2))
+        spread(B1_ROW, b1_bc, range(0, 4), scalar_only=True)
+        project(0)
+        negative_mean(0)
+        sum_of_squares(0)
+        centre_and_scale(0)
+        inverse_deviation(0)
+        spread(B1_ROW, b1_bc, range(4, 8), scalar_only=True)
+        project(1)
+        grouped_a = turn_attn(2)
+        negative_mean(1)
+        centre_and_scale(1)
+        finish_norm(0)
+        quantise_attn(2, grouped_a)
+        turn_h2(0)
+        sum_of_squares(1)
+        inverse_deviation(1)
+        add_bias_to_residual(3)
+
+        for s in range(2, TILES + 2):
             if is_tile(s + 1):
-                quantise(grouped_a, a_codes[:, s + 1, :], a_planes[:, s + 1, :])
-                add_bias_to_residual(s + 1)
+                grouped_a = turn_attn(s + 1)
+            if is_tile(s - 3):
+                gelu_and_store(s - 3, 1)
+            quantise_h2(s - 2)
+            if is_tile(s + 1):
+                quantise_attn(s + 1, grouped_a)
             if is_tile(s):
                 project(s)
-            if is_tile(s) and not is_tile(s - 2):
-                statistics(s)
-            if is_tile(s - 2):
-                up_project(
-                    s - 2, 0, by_bank=(s - 2 == LAST),
-                    after_first_bank=(lambda: statistics(s)) if is_tile(s) else None,
-                )
-                if s - 2 != LAST:
-                    gelu_and_store(s - 2, 0)
+            up_bank(s - 2, 0)
+            if is_tile(s):
+                negative_mean(s)
+                sum_of_squares(s)
+                centre_and_scale(s)
+                inverse_deviation(s)
+            if is_tile(s + 2):
+                add_bias_to_residual(s + 2)
+            for c in range(1, 4):
+                up_bank(s - 2, c)
+            gelu_and_store(s - 2, 0)
             if is_tile(s - 1):
                 finish_norm(s - 1)
-            if is_tile(s - 2):
-                up_project(s - 2, 1, by_bank=(s - 2 == LAST))
-            if s == -1:
-                spread(G_ROW, g_bc)
-                spread(B_ROW, b_bc)
-            if s == 0:
-                spread(B1_ROW, b1_bc)
+            for c in range(4, 8):
+                up_bank(s - 2, c)
+            if is_tile(s - 1):
+                turn_h2(s - 1)

@@ -169,6 +169,7 @@ def tile_transformerblock_pb_kernel(
         LAST = TILES - 1
         RESIDUAL_ON_VECTOR = (0,)
         CENTRE_ON_VECTOR = (0,)
+        VECTOR_SHARE = 256
         BY_BANK_FROM = (LAST, 0)
 
         xb_of = {}
@@ -221,20 +222,28 @@ def tile_transformerblock_pb_kernel(
             )
             ssq_of[i] = ssq
 
+        def centre_and_scale_on_vector(i, cols):
+            nc.vector.scalar_tensor_tensor(
+                out=scaled_of[i][:, cols], in0=xmid_of[i][:, cols], scalar=neg_mean_of[i][:], in1=g_bc[:, cols],
+                op0=ALU.add, op1=ALU.mult,
+            )
+
         def centre_and_scale(i):
             scaled = work.tile([P, D], F32, bufs=3)
-            if i in CENTRE_ON_VECTOR:
-                nc.vector.scalar_tensor_tensor(
-                    out=scaled[:], in0=xmid_of[i][:], scalar=neg_mean_of[i][:], in1=g_bc[:],
-                    op0=ALU.add, op1=ALU.mult,
-                )
-            else:
-                nc.gpsimd.tensor_scalar(
-                    out=scaled[:], in0=xmid_of[i][:], scalar1=neg_mean_of[i][:], scalar2=1.0,
-                    op0=ALU.add, op1=ALU.mult,
-                )
-                nc.gpsimd.tensor_tensor(out=scaled[:], in0=scaled[:], in1=g_bc[:], op=ALU.mult)
             scaled_of[i] = scaled
+            if i in CENTRE_ON_VECTOR:
+                centre_and_scale_on_vector(i, slice(0, D))
+            else:
+                cols = slice(0, D - VECTOR_SHARE)
+                nc.gpsimd.tensor_scalar(
+                    out=scaled[:, cols], in0=xmid_of[i][:, cols], scalar1=neg_mean_of[i][:], scalar2=1.0,
+                    op0=ALU.add, op1=ALU.mult,
+                )
+                nc.gpsimd.tensor_tensor(out=scaled[:, cols], in0=scaled[:, cols], in1=g_bc[:, cols], op=ALU.mult)
+
+        def vector_share(i):
+            if i not in CENTRE_ON_VECTOR:
+                centre_and_scale_on_vector(i, slice(D - VECTOR_SHARE, D))
 
         def inverse_deviation(i):
             var_eps = stats.tile([P, 1], F32)
@@ -316,6 +325,7 @@ def tile_transformerblock_pb_kernel(
         negative_mean(1)
         centre_and_scale(1)
         finish_norm(0)
+        vector_share(1)
         quantise_attn(2, grouped_a)
         turn_h2(0)
         sum_of_squares(1)
@@ -340,8 +350,11 @@ def tile_transformerblock_pb_kernel(
                 inverse_deviation(s)
             if is_tile(s + 2):
                 add_bias_to_residual(s + 2)
-            for c in range(1, 4):
-                up_bank(s - 2, c)
+            up_bank(s - 2, 1)
+            if is_tile(s):
+                vector_share(s)
+            up_bank(s - 2, 2)
+            up_bank(s - 2, 3)
             gelu_and_store(s - 2, 0)
             if is_tile(s - 1):
                 finish_norm(s - 1)

@@ -120,21 +120,25 @@ def tile_transformerblock_pb_kernel(
 
         def warm_up(count):
             for n in range(count):
-                acc = psum_up.tile([P, BANK], F32, tag="up")
+                acc = psum_mid.tile([P, BANK], F32)
                 nc.tensor.matmul(out=acc[:], lhsT=zeros[:, 0:P], rhs=zeros[:], start=True, stop=True)
+
+        def spread_row(r):
+            acc = psum_up.tile([P, BANK], F32, tag="up")
+            nc.tensor.matmul(
+                out=acc[:], lhsT=ident_bf[:, r : r + 1].to_broadcast([P, P]), rhs=vec_rows[:], start=True, stop=True
+            )
+            return acc
+
+        def keep_row(acc, dest, j, on_scalar):
+            if on_scalar:
+                nc.scalar.copy(out=dest[:, j * BANK : (j + 1) * BANK], in_=acc[:])
+            else:
+                nc.vector.tensor_copy(out=dest[:, j * BANK : (j + 1) * BANK], in_=acc[:])
 
         def spread(first_row, dest, banks, scalar_only=False):
             for j in banks:
-                r = first_row + j
-                acc = psum_up.tile([P, BANK], F32, tag="up")
-                nc.tensor.matmul(
-                    out=acc[:], lhsT=ident_bf[:, r : r + 1].to_broadcast([P, P]), rhs=vec_rows[:],
-                    start=True, stop=True,
-                )
-                if r % 2 == 0 or scalar_only:
-                    nc.scalar.copy(out=dest[:, j * BANK : (j + 1) * BANK], in_=acc[:])
-                else:
-                    nc.vector.tensor_copy(out=dest[:, j * BANK : (j + 1) * BANK], in_=acc[:])
+                keep_row(spread_row(first_row + j), dest, j, j % 2 == 0 or scalar_only)
 
         def transpose_rows(rows):
             words = rows.bitcast(F32)
@@ -208,9 +212,8 @@ def tile_transformerblock_pb_kernel(
         def negative_mean(i):
             neg_mean = stats.tile([P, 1], F32)
             parts = stats.tile([P, D // BANK], F32)
-            nc.vector.tensor_scalar(
-                out=parts[:], in0=sums_of[i][:], scalar1=-1.0 / D, scalar2=None, op0=ALU.mult, op1=ALU.add,
-                accum_out=neg_mean[:],
+            nc.scalar.activation(
+                out=parts[:], in_=sums_of[i][:], func=ACT.Copy, scale=-1.0 / D, accum_out=neg_mean[:]
             )
             neg_mean_of[i] = neg_mean
 
@@ -305,43 +308,57 @@ def tile_transformerblock_pb_kernel(
         def quantise_attn(i, grouped):
             quantise(grouped, a_codes[:, i, :], a_planes[:, i, :])
 
-        warm_up(5)
+        warm_up(4)
         quantise_attn(0, turn_attn(0))
         spread(BO_ROW, bo_bc, range(2))
+        spread(G_ROW, g_bc, range(2))
+        grouped_a = turn_attn(1)
+        spread(B_ROW, b_bc, range(2))
         for i in range(3):
             add_bias_to_residual(i)
-        quantise_attn(1, turn_attn(1))
-        spread(G_ROW, g_bc, range(2))
-        spread(B_ROW, b_bc, range(2))
+        quantise_attn(1, grouped_a)
         spread(B1_ROW, b1_bc, range(0, 4), scalar_only=True)
         project(0)
+        project(1)
         negative_mean(0)
         sum_of_squares(0)
         centre_and_scale(0)
         inverse_deviation(0)
-        spread(B1_ROW, b1_bc, range(4, 8), scalar_only=True)
-        project(1)
-        grouped_a = turn_attn(2)
         negative_mean(1)
-        centre_and_scale(1)
-        finish_norm(0)
-        vector_share(1)
-        quantise_attn(2, grouped_a)
-        turn_h2(0)
         sum_of_squares(1)
+        centre_and_scale(1)
+        vector_share(1)
+        grouped_a = turn_attn(2)
+        late_rows = {}
+        for j in range(4, 8):
+            late_rows[j] = spread_row(B1_ROW + j)
+        keep_row(late_rows[4], b1_bc, 4, True)
+        keep_row(late_rows[5], b1_bc, 5, True)
+        finish_norm(0)
+        quantise_attn(2, grouped_a)
+        keep_row(late_rows[6], b1_bc, 6, False)
+        keep_row(late_rows[7], b1_bc, 7, False)
+        warm_up(4)
+        turn_h2(0)
         inverse_deviation(1)
         add_bias_to_residual(3)
 
         for s in range(2, TILES + 2):
+            last_norm = s == LAST + 1
+            if last_norm:
+                warm_up(5)
             if is_tile(s + 1):
                 grouped_a = turn_attn(s + 1)
             if is_tile(s - 3):
                 gelu_and_store(s - 3, 1)
-            quantise_h2(s - 2)
+            if s - 2 != LAST:
+                quantise_h2(s - 2)
             if is_tile(s + 1):
                 quantise_attn(s + 1, grouped_a)
             if is_tile(s):
                 project(s)
+            if last_norm:
+                finish_norm(LAST)
             up_bank(s - 2, 0)
             if is_tile(s):
                 negative_mean(s)
@@ -355,10 +372,13 @@ def tile_transformerblock_pb_kernel(
                 vector_share(s)
             up_bank(s - 2, 2)
             up_bank(s - 2, 3)
+            if last_norm:
+                turn_h2(LAST)
+                quantise_h2(LAST)
             gelu_and_store(s - 2, 0)
-            if is_tile(s - 1):
+            if is_tile(s - 1) and not last_norm:
                 finish_norm(s - 1)
             for c in range(4, 8):
                 up_bank(s - 2, c)
-            if is_tile(s - 1):
+            if is_tile(s - 1) and not last_norm:
                 turn_h2(s - 1)

@@ -68,6 +68,8 @@ def tile_transformerblock_pb_kernel(
 
         zeros = keep.tile([P, BANK], BF16)
         nc.vector.memset(zeros[:], 0.0)
+        first_gelu = keep.tile([P, 1], F32)
+        nc.scalar.activation(out=first_gelu[:], in_=zeros[:, 0:1], func=ACT.Gelu)
         make_identity(nc, ident[:])
         make_identity(nc, ident_bf[:])
         nc.gpsimd.memset(neg_half[:], -0.5)
@@ -381,4 +383,5 @@ def tile_transformerblock_pb_kernel(
             for c in range(4, 8):
                 up_bank(s - 2, c)
             if is_tile(s - 1) and not last_norm:
+                warm_up(2)
                 turn_h2(s - 1)

from contextlib import ExitStack

import concourse.mybir as mybir
from concourse.masks import make_identity

F32 = mybir.dt.float32
BF16 = mybir.dt.bfloat16
I32 = mybir.dt.int32
U32 = mybir.dt.uint32
U8 = mybir.dt.uint8
FP8X4 = mybir.dt.float8_e4m3fn_x4
ALU = mybir.AluOpType
ACT = mybir.ActivationFunctionType

P = 128
TOKENS = 1024
TILES = TOKENS // P
D = 1024
F = 4096
K_PASS = 512
PASSES = D // K_PASS
BANK = 512
Z_COLS = 2048
EPS = 1e-5

FLOPS = 2 * TOKENS * D * (D + F)


def tile_transformerblock_pb_kernel(
    tc, attn, x, w_out_words, w_out_scales, b_out, ln2_g, ln2_b, w1_words, w1_scales, b1, out_0, out_1
):
    nc = tc.nc

    attn_v = attn.flatten_outer_dims().rearrange("(p i) k -> p i k", i=TILES)
    x_v = x.flatten_outer_dims().rearrange("(p i) k -> p i k", i=TILES)
    xmid_v = out_0.flatten_outer_dims().rearrange("(p i) n -> p i n", i=TILES)
    hid_v = out_1.flatten_outer_dims().rearrange("(p i) n -> p i n", i=TILES)

    with ExitStack() as stack:
        keep = stack.enter_context(tc.tile_pool(name="keep", bufs=1))
        work = stack.enter_context(tc.tile_pool(name="work", bufs=2))
        stats = stack.enter_context(tc.tile_pool(name="stats", bufs=4))
        zpool = stack.enter_context(tc.tile_pool(name="zpool", bufs=5))
        psum_t = stack.enter_context(tc.psum_pool(name="psum_t", bufs=2))
        psum_mid = stack.enter_context(tc.psum_pool(name="psum_mid", bufs=2))
        psum_up = stack.enter_context(tc.psum_pool(name="psum_up", bufs=4))
        stack.enter_context(tc.manual_schedule())

        attn_sb = keep.tile([P, TILES, D], BF16)
        x_sb = keep.tile([P, TILES, D], BF16)
        wo_sb = keep.tile([P, PASSES, D], I32, align_bytes=64)
        w1_sb = keep.tile([P, PASSES, F], I32, align_bytes=64)
        wo_planes = keep.tile([P, D], U8, align_bytes=64)
        w1_planes = keep.tile([P, F], U8, align_bytes=64)
        bo_bc = keep.tile([P, D], BF16)
        g_bc = keep.tile([P, D], BF16)
        b_bc = keep.tile([P, D], BF16)
        b1_bc = keep.tile([P, F], BF16)
        a_codes = keep.tile([P, TILES, PASSES * P], U32, align_bytes=64)
        a_planes = keep.tile([P, TILES, PASSES * P], U8, align_bytes=64)
        h_codes = keep.tile([P, TILES, PASSES * P], U32, align_bytes=64)
        h_planes = keep.tile([P, TILES, PASSES * P], U8, align_bytes=64)
        ident = keep.tile([P, P], F32)
        ident_bf = keep.tile([P, P], BF16)
        neg_half = keep.tile([P, 1], F32)
        vec_rows = keep.tile([P, BANK], BF16)
        B1_ROW, BO_ROW, G_ROW, B_ROW = 0, 8, 10, 12

        zeros = keep.tile([P, BANK], BF16)
        nc.vector.memset(zeros[:], 0.0)
        first_gelu = keep.tile([P, 1], F32)
        nc.scalar.activation(out=first_gelu[:], in_=zeros[:, 0:1], func=ACT.Gelu)
        make_identity(nc, ident[:])
        make_identity(nc, ident_bf[:])
        nc.gpsimd.memset(neg_half[:], -0.5)
        nc.vector.memset(vec_rows[:], 0.0)
        nc.vector.memset(wo_planes[:].bitcast(I32), 0)
        nc.vector.memset(w1_planes[:].bitcast(I32), 0)

        def load_planes(planes, scales):
            for q in range(4):
                nc.sync.dma_start(
                    out=planes[32 * q : 32 * q + 4 * PASSES, :].bitcast(I32),
                    in_=scales[:, 4 * q : 4 * q + 4, :].bitcast(I32),
                )

        def load_words(words_sb, words, g, cols):
            nc.sync.dma_start(
                out=words_sb[:, g, cols],
                in_=words[g].rearrange("p n t -> p (n t)").bitcast(I32)[:, cols],
            )

        def load_attn(tiles):
            nc.sync.dma_start(out=attn_sb[:, tiles, :], in_=attn_v[:, tiles, :])

        def load_x(tiles):
            nc.sync.dma_start(out=x_sb[:, tiles, :], in_=x_v[:, tiles, :])

        def load_vector(first_row, vector):
            rows = vector.rearrange("(r c) -> r c", c=BANK)
            nc.sync.dma_start(out=vec_rows[first_row : first_row + rows.shape[0], :], in_=rows)

        load_attn(slice(0, 2))
        load_vector(BO_ROW, b_out)
        load_vector(G_ROW, ln2_g)
        load_vector(B_ROW, ln2_b)
        load_vector(B1_ROW, b1)
        load_x(slice(0, 2))
        load_planes(wo_planes, w_out_scales)
        for g in range(PASSES):
            load_words(wo_sb, w_out_words, g, slice(0, D))
        load_x(slice(2, 4))
        load_attn(slice(2, 4))
        load_planes(w1_planes, w1_scales)
        for half in range(2):
            for g in range(PASSES):
                load_words(w1_sb, w1_words, g, slice(half * F // 2, (half + 1) * F // 2))
        load_attn(slice(4, 6))
        load_x(slice(4, 6))
        load_attn(slice(6, TILES))
        load_x(slice(6, TILES))

        def warm_up(count):
            for n in range(count):
                acc = psum_mid.tile([P, BANK], F32)
                nc.tensor.matmul(out=acc[:], lhsT=zeros[:, 0:P], rhs=zeros[:], start=True, stop=True)

        def spread_row(r):
            acc = psum_up.tile([P, BANK], F32, tag="up")
            nc.tensor.matmul(
                out=acc[:], lhsT=ident_bf[:, r : r + 1].to_broadcast([P, P]), rhs=vec_rows[:], start=True, stop=True
            )
            return acc

        def keep_row(acc, dest, j, on_scalar):
            if on_scalar:
                nc.scalar.copy(out=dest[:, j * BANK : (j + 1) * BANK], in_=acc[:])
            else:
                nc.vector.tensor_copy(out=dest[:, j * BANK : (j + 1) * BANK], in_=acc[:])

        def spread(first_row, dest, banks, scalar_only=False):
            for j in banks:
                keep_row(spread_row(first_row + j), dest, j, j % 2 == 0 or scalar_only)

        def transpose_rows(rows):
            words = rows.bitcast(F32)
            tp = psum_t.tile([P, PASSES, 2, P], F32)
            for g in range(PASSES):
                for u in range(2):
                    nc.tensor.transpose(tp[:, g, u, :], words[:, 256 * g + u : 256 * (g + 1) : 2], ident[:])
            return tp

        def regroup(tp):
            grouped = work.tile([P, PASSES, P, 4], BF16, align_bytes=64, bufs=4)
            nc.scalar.copy(out=grouped[:].bitcast(F32), in_=tp[:].rearrange("p g u r -> p g r u"))
            return grouped

        def quantise(grouped, codes, planes):
            nc.vector.quantize_mx(
                out=codes.bitcast(FP8X4), scales=planes, in_=grouped[:].rearrange("p g r t -> p (g r t)")
            )

        def mx_product(acc, codes, planes, w_sb, w_planes, cols):
            for g in range(PASSES):
                nc.tensor.matmul_mx(
                    out=acc,
                    lhsT=codes[:, g * P : (g + 1) * P].bitcast(FP8X4),
                    lhsT_scale=planes[:, g * P : (g + 1) * P],
                    rhs=w_sb[:, g, cols].bitcast(FP8X4),
                    rhs_scale=w_planes[4 * g : P, cols],
                    start=(g == 0),
                    stop=(g == PASSES - 1),
                )

        LAST = TILES - 1
        RESIDUAL_ON_VECTOR = (0,)
        CENTRE_ON_VECTOR = (0,)
        VECTOR_SHARE = 256
        BY_BANK_FROM = (LAST, 0)

        xb_of = {}
        xmid_of = {}
        sums_of = {}
        neg_mean_of = {}
        ssq_of = {}
        scaled_of = {}
        rstd_of = {}
        h2_of = {}
        grouped_of = {}
        z_of = {}
        acc_of = {}

        def add_bias_to_residual(i):
            xb = work.tile([P, D], F32, bufs=3)
            engine = nc.vector if i in RESIDUAL_ON_VECTOR else nc.gpsimd
            engine.tensor_tensor(out=xb[:], in0=x_sb[:, i, :], in1=bo_bc[:], op=ALU.add)
            xb_of[i] = xb

        def project(i):
            xmid = work.tile([P, D], F32, bufs=3)
            sums = stats.tile([P, D // BANK], F32)
            for h in range(D // BANK):
                cols = slice(h * BANK, (h + 1) * BANK)
                acc = psum_mid.tile([P, BANK], F32)
                mx_product(acc[:], a_codes[:, i, :], a_planes[:, i, :], wo_sb, wo_planes, cols)
                nc.vector.scalar_tensor_tensor(
                    out=xmid[:, cols], in0=acc[:], scalar=0.0, in1=xb_of[i][:, cols],
                    op0=ALU.add, op1=ALU.add, accum_out=sums[:, h : h + 1],
                )
            nc.sync.dma_start(out=xmid_v[:, i, :], in_=xmid[:])
            xmid_of[i] = xmid
            sums_of[i] = sums

        def negative_mean(i):
            neg_mean = stats.tile([P, 1], F32)
            parts = stats.tile([P, D // BANK], F32)
            nc.scalar.activation(
                out=parts[:], in_=sums_of[i][:], func=ACT.Copy, scale=-1.0 / D, accum_out=neg_mean[:]
            )
            neg_mean_of[i] = neg_mean

        def sum_of_squares(i):
            squares = work.tile([P, D], BF16)
            ssq = stats.tile([P, 1], F32)
            nc.scalar.activation(
                out=squares[:], in_=xmid_of[i][:], func=ACT.Square, bias=neg_mean_of[i][:], accum_out=ssq[:]
            )
            ssq_of[i] = ssq

        def centre_and_scale_on_vector(i, cols):
            nc.vector.scalar_tensor_tensor(
                out=scaled_of[i][:, cols], in0=xmid_of[i][:, cols], scalar=neg_mean_of[i][:], in1=g_bc[:, cols],
                op0=ALU.add, op1=ALU.mult,
            )

        def centre_and_scale(i):
            scaled = work.tile([P, D], F32, bufs=3)
            scaled_of[i] = scaled
            if i in CENTRE_ON_VECTOR:
                centre_and_scale_on_vector(i, slice(0, D))
            else:
                cols = slice(0, D - VECTOR_SHARE)
                nc.gpsimd.tensor_scalar(
                    out=scaled[:, cols], in0=xmid_of[i][:, cols], scalar1=neg_mean_of[i][:], scalar2=1.0,
                    op0=ALU.add, op1=ALU.mult,
                )
                nc.gpsimd.tensor_tensor(out=scaled[:, cols], in0=scaled[:, cols], in1=g_bc[:, cols], op=ALU.mult)

        def vector_share(i):
            if i not in CENTRE_ON_VECTOR:
                centre_and_scale_on_vector(i, slice(D - VECTOR_SHARE, D))

        def inverse_deviation(i):
            var_eps = stats.tile([P, 1], F32)
            nc.gpsimd.tensor_scalar(
                out=var_eps[:], in0=ssq_of[i][:], scalar1=1.0 / D, scalar2=EPS, op0=ALU.mult, op1=ALU.add
            )
            rstd = stats.tile([P, 1], F32)
            nc.gpsimd.tensor_tensor(out=rstd[:], in0=var_eps[:], in1=neg_half[:], op=ALU.pow)
            rstd_of[i] = rstd

        def finish_norm(i):
            h2 = work.tile([P, D], BF16)
            nc.vector.scalar_tensor_tensor(
                out=h2[:], in0=scaled_of[i][:], scalar=rstd_of[i][:], in1=b_bc[:], op0=ALU.mult, op1=ALU.add
            )
            h2_of[i] = h2

        def turn_h2(i):
            grouped_of[i] = regroup(transpose_rows(h2_of[i][:]))

        def quantise_h2(i):
            quantise(grouped_of[i], h_codes[:, i, :], h_planes[:, i, :])

        def up_passes(i, c):
            acc = psum_up.tile([P, BANK], F32, tag="up")
            mx_product(acc[:], h_codes[:, i, :], h_planes[:, i, :], w1_sb, w1_planes, slice(c * BANK, (c + 1) * BANK))
            acc_of[(i, c)] = acc

        def add_b1(i, c):
            half, quarter = divmod(c, Z_COLS // BANK)
            if quarter == 0:
                z = zpool.tile([P, Z_COLS], F32)
                z_of[(i, half)] = z
            z = z_of[(i, half)]
            cols = slice(c * BANK, (c + 1) * BANK)
            z_cols = z[:, quarter * BANK : (quarter + 1) * BANK]
            nc.vector.tensor_tensor(out=z_cols, in0=acc_of[(i, c)][:], in1=b1_bc[:, cols], op=ALU.add)
            if (i, c) >= BY_BANK_FROM:
                nc.scalar.activation(out=z_cols, in_=z_cols, func=ACT.Gelu)
                nc.sync.dma_start(out=hid_v[:, i, cols], in_=z_cols)

        def up_bank(i, c):
            up_passes(i, c)
            add_b1(i, c)

        def gelu_and_store(i, half):
            if (i, half * (Z_COLS // BANK)) >= BY_BANK_FROM:
                return
            z = z_of[(i, half)]
            nc.scalar.activation(out=z[:], in_=z[:], func=ACT.Gelu)
            nc.sync.dma_start(out=hid_v[:, i, half * Z_COLS : (half + 1) * Z_COLS], in_=z[:])

        def is_tile(i):
            return 0 <= i < TILES

        def turn_attn(i):
            return regroup(transpose_rows(attn_sb[:, i, :]))

        def quantise_attn(i, grouped):
            quantise(grouped, a_codes[:, i, :], a_planes[:, i, :])

        warm_up(4)
        quantise_attn(0, turn_attn(0))
        spread(BO_ROW, bo_bc, range(2))
        spread(G_ROW, g_bc, range(2))
        grouped_a = turn_attn(1)
        spread(B_ROW, b_bc, range(2))
        for i in range(3):
            add_bias_to_residual(i)
        quantise_attn(1, grouped_a)
        spread(B1_ROW, b1_bc, range(0, 4), scalar_only=True)
        project(0)
        project(1)
        negative_mean(0)
        sum_of_squares(0)
        centre_and_scale(0)
        inverse_deviation(0)
        negative_mean(1)
        sum_of_squares(1)
        centre_and_scale(1)
        vector_share(1)
        grouped_a = turn_attn(2)
        late_rows = {}
        for j in range(4, 8):
            late_rows[j] = spread_row(B1_ROW + j)
        keep_row(late_rows[4], b1_bc, 4, True)
        keep_row(late_rows[5], b1_bc, 5, True)
        finish_norm(0)
        quantise_attn(2, grouped_a)
        keep_row(late_rows[6], b1_bc, 6, False)
        keep_row(late_rows[7], b1_bc, 7, False)
        warm_up(4)
        turn_h2(0)
        inverse_deviation(1)
        add_bias_to_residual(3)

        for s in range(2, TILES + 2):
            last_norm = s == LAST + 1
            if last_norm:
                warm_up(5)
            if is_tile(s + 1):
                grouped_a = turn_attn(s + 1)
            if is_tile(s - 3):
                gelu_and_store(s - 3, 1)
            if s - 2 != LAST:
                quantise_h2(s - 2)
            if is_tile(s + 1):
                quantise_attn(s + 1, grouped_a)
            if is_tile(s):
                project(s)
            if last_norm:
                finish_norm(LAST)
            up_bank(s - 2, 0)
            if is_tile(s):
                negative_mean(s)
                sum_of_squares(s)
                centre_and_scale(s)
                inverse_deviation(s)
            if is_tile(s + 2):
                add_bias_to_residual(s + 2)
            up_bank(s - 2, 1)
            if is_tile(s):
                vector_share(s)
            up_bank(s - 2, 2)
            up_bank(s - 2, 3)
            if last_norm:
                turn_h2(LAST)
                quantise_h2(LAST)
            gelu_and_store(s - 2, 0)
            if is_tile(s - 1) and not last_norm:
                finish_norm(s - 1)
            for c in range(4, 8):
                up_bank(s - 2, c)
            if is_tile(s - 1) and not last_norm:
                warm_up(2)
                turn_h2(s - 1)
